import numpy as np
import ml_dtypes


def mxq(x, axis, fmt="e4m3"):
    dtype, down = {"e4m3": (ml_dtypes.float8_e4m3fn, 7), "e5m2": (ml_dtypes.float8_e5m2, 14)}[fmt]
    v = np.moveaxis(np.asarray(x, np.float32).astype(ml_dtypes.bfloat16).astype(np.float64), axis, -1)
    blocks = v.reshape(v.shape[:-1] + (-1, 32))
    amax = np.abs(blocks).max(-1, keepdims=True)
    byte = np.maximum(np.where(amax > 0, np.frexp(amax)[1] - 1 + 127, 0) - down, 1)
    scale = np.exp2(byte - 127.0)
    codes = (blocks / scale).astype(np.float32).astype(dtype).astype(np.float64)
    return np.moveaxis((codes * scale).reshape(v.shape), -1, axis)


WIDE = False


def mx_kscale(k):
    if not WIDE:
        return np.ones(k)
    levels = np.array([10, -10, 5, -5, 0])
    a = np.random.permutation(np.resize(levels, k // 512 * 4)).reshape(k // 512, 4)
    idx = np.arange(k)
    return np.exp2(a[idx // 512, idx % 128 // 32])


BF16 = ml_dtypes.bfloat16


def bf(x):
    return np.asarray(x, np.float32).astype(BF16)


def f64(x):
    return np.asarray(x).astype(np.float64)


E2M1 = np.array([0.0, 0.5, 1.0, 1.5, 2.0, 3.0, 4.0, 6.0, -0.0, -0.5, -1.0, -1.5, -2.0, -3.0, -4.0, -6.0])


def pack_weight(w, fmt):
    k, n = w.shape
    w = f64(bf(w)).reshape(k // 32, 32, n)
    amax = np.abs(w).max(1)
    if fmt == "e4m3":
        byte = np.frexp(amax)[1] - 1 + 127 - 7
    else:
        mant, ex = np.frexp(amax / 6.0)
        byte = np.where(mant > 0.5, ex, ex - 1) + 127
    byte = np.clip(np.where(amax > 0, byte, 1), 1, 254)
    scaled = (w * np.exp2(127.0 - byte)[:, None, :]).reshape(k, n).astype(np.float32)
    by_word = np.ascontiguousarray(scaled.reshape(k // 512, 128, 4, n).transpose(0, 1, 3, 2))
    if fmt == "e4m3":
        words = by_word.astype(ml_dtypes.float8_e4m3fn).view(np.uint8)
    else:
        c = by_word.astype(ml_dtypes.float4_e2m1fn).view(np.uint8) & 0xF
        words = c[..., 0::2] | (c[..., 1::2] << 4)
    return np.ascontiguousarray(words), np.ascontiguousarray(byte.astype(np.uint8).reshape(k // 512, 16, n))


def unpack_weight(words, scales, fmt):
    g, p, n, _ = words.shape
    if fmt == "e4m3":
        vals = np.ascontiguousarray(words).view(ml_dtypes.float8_e4m3fn).astype(np.float64)
    else:
        nib = np.empty((g, p, n, 4), np.uint8)
        nib[..., 0::2] = words & 0xF
        nib[..., 1::2] = words >> 4
        vals = E2M1[nib]
    vals = vals * np.repeat(np.exp2(scales.astype(np.float64) - 127.0), 8, axis=1)[..., None]
    return vals.transpose(0, 1, 3, 2).reshape(g * 512, n)


B, H = 128, 3072
DMN_FACTOR = 0.5
FMT = "e4m3"


def sigmoid(v):
    return 1.0 / (1.0 + np.exp(-v))


def setup_inputs():
    s = mx_kscale(H)
    x = bf(np.random.standard_normal((B, H)) * s)
    w = np.random.standard_normal((H, H)) / np.sqrt(H) / s[None, :]
    b = bf(np.random.standard_normal(H) * 0.1)
    plasticity_modulation = bf(np.random.uniform(0.0, 1.0, H) / s)
    cm = np.random.uniform(0.0, 1.0, (H, H)) * 6.0 * np.sqrt(H)
    W_words, W_scales = pack_weight(w.T, FMT)
    cm_words, cm_scales = pack_weight(cm.T, FMT)
    return {"x": x,
            "W_words": W_words,
            "W_scales": W_scales,
            "b": b,
            "plasticity_modulation": plasticity_modulation,
            "connectivity_mask_words": cm_words,
            "connectivity_mask_scales": cm_scales}


def reference(x, W_words, W_scales, b, plasticity_modulation, connectivity_mask_words, connectivity_mask_scales):
    x = f64(x)
    hn = x.shape[1]
    bdnf_effect = sigmoid((mxq(x, 1, "e4m3") @ unpack_weight(W_words, W_scales, FMT)) + f64(b))
    xs = x * f64(plasticity_modulation)
    g = mxq(xs, 1, "e4m3") @ unpack_weight(connectivity_mask_words, connectivity_mask_scales, FMT)
    fi = xs * g * (DMN_FACTOR / hn)
    return xs + bdnf_effect * fi

@@ -1,0 +1,230 @@
+from contextlib import ExitStack
+
+import concourse.mybir as mybir
+from concourse.masks import make_identity
+
+F32 = mybir.dt.float32
+BF16 = mybir.dt.bfloat16
+U8 = mybir.dt.uint8
+U32 = mybir.dt.uint32
+I32 = mybir.dt.int32
+FP8X4 = mybir.dt.float8_e4m3fn_x4
+ALU = mybir.AluOpType
+ACT = mybir.ActivationFunctionType
+
+P = 128
+H = 3072
+G = 6
+NB = 512
+FLOPS = 2 * 2 * 128 * 3072 * 3072
+CHUNKS = [(0, 2048), (2048, 512), (2560, 512)]
+W_SCALES_ON = "gpsimd"
+WEAVE = 2
+PIN = True
+TWO_BY = "row"
+
+
+def tile_neuroplasticitymodule_w_kernel(
+    tc,
+    x,
+    W_words,
+    W_scales,
+    b,
+    plasticity_modulation,
+    connectivity_mask_words,
+    connectivity_mask_scales,
+    out,
+):
+    nc = tc.nc
+    with ExitStack() as ctx:
+        keep = ctx.enter_context(tc.tile_pool(name="keep", bufs=1))
+        psum = ctx.enter_context(tc.psum_pool(name="psum", bufs=1))
+        if PIN:
+            ctx.enter_context(tc.manual_schedule())
+
+        def bank(i, shape, name):
+            return psum.tile(shape, F32, name=name, tag="bank%d" % i)
+
+        x_sb = keep.tile([P, H], BF16, name="x_sb")
+        z = keep.tile([P, NB], BF16, name="z")
+        warm = keep.tile([P, 1], F32, name="warm")
+        warm2 = keep.tile([P, 1], F32, name="warm2")
+        ident32 = keep.tile([P, P], F32, name="ident32")
+        identb = keep.tile([P, P], BF16, name="identb")
+        tw = keep.tile([P, H], U8, name="tw", align_bytes=64)
+        t45 = keep.tile([P, H], U8, name="t45", align_bytes=64)
+        tcm = keep.tile([P, H], U8, name="tcm", align_bytes=64)
+        w_sb = [keep.tile([P, H], U32, name="w%d" % g, align_bytes=64) for g in range(G)]
+        c_sb = [
+            [keep.tile([P, wd], U32, name="c%d_%d" % (ci, g), align_bytes=64) for g in range(G)]
+            for ci, (c0, wd) in enumerate(CHUNKS)
+        ]
+        xg = keep.tile([P, H], BF16, name="xg", align_bytes=64)
+        xsg = keep.tile([P, H], BF16, name="xsg", align_bytes=64)
+        xc = keep.tile([P, H // 4], U32, name="xc", align_bytes=64)
+        xp = keep.tile([P, H // 4], U8, name="xp", align_bytes=64)
+        xsc = keep.tile([P, H // 4], U32, name="xsc", align_bytes=64)
+        xsp = keep.tile([P, H // 4], U8, name="xsp", align_bytes=64)
+        pmt = keep.tile([P, 4 * G], BF16, name="pmt")
+        xs32 = [keep.tile([P, NB], F32, name="xs32_%d" % j) for j in range(G)]
+        ba = [keep.tile([P, NB], F32, name="ba%d" % j) for j in range(G)]
+
+        nc.vector.memset(warm[:], 0.0)
+        nc.vector.memset(z[:], 0.0)
+        for t in (tw, t45, tcm):
+            nc.vector.memset(t[:].bitcast(I32), 0)
+
+        def four_planes(eng, dt, t, scales):
+            return [
+                (eng, t[32 * q : 32 * q + 16, :].bitcast(dt), scales[0:4, 4 * q : 4 * q + 4, :].bitcast(dt))
+                for q in range(4)
+            ]
+
+        def two_planes(eng, dt, k0, scales, by):
+            if by == "quadrant":
+                return [
+                    (eng, t45[32 * q + k0 : 32 * q + k0 + 8, :].bitcast(dt), scales[4:6, 4 * q : 4 * q + 4, :].bitcast(dt))
+                    for q in range(4)
+                ]
+            return [
+                (eng, t45[k0 + 4 * (g - 4) + r : P : 32, :].bitcast(dt), scales[g, r : 16 : 4, :].bitcast(dt))
+                for g in (4, 5)
+                for r in range(4)
+            ]
+
+        def start(d):
+            d[0].dma_start(out=d[1], in_=d[2])
+
+        bigs = [
+            (nc.sync, w_sb[g][:].bitcast(I32), W_words[g].rearrange("p n t -> p (n t)").bitcast(I32)) for g in range(G)
+        ] + [
+            (
+                nc.sync,
+                c_sb[ci][g][:].bitcast(I32),
+                connectivity_mask_words[g].rearrange("p n t -> p (n t)")[:, 4 * c0 : 4 * (c0 + wd)].bitcast(I32),
+            )
+            for ci, (c0, wd) in enumerate(CHUNKS)
+            for g in range(G)
+        ]
+        smalls = []
+        if W_SCALES_ON == "sync":
+            smalls += four_planes(nc.sync, I32, tw, W_scales) + two_planes(nc.sync, I32, 0, W_scales, TWO_BY)
+        smalls += four_planes(nc.sync, I32, tcm, connectivity_mask_scales)
+        smalls += two_planes(nc.sync, I32, 8, connectivity_mask_scales, TWO_BY)
+
+        nc.sync.dma_start(out=x_sb[:], in_=x)
+        if WEAVE == 0:
+            for d in smalls:
+                start(d)
+            for d in bigs:
+                start(d)
+        else:
+            si = 0
+            for d in bigs:
+                start(d)
+                for d2 in smalls[si : si + WEAVE]:
+                    start(d2)
+                si += WEAVE
+
+        nc.scalar.dma_start(out=z[0:G, :], in_=plasticity_modulation.rearrange("(g c) -> g c", c=NB))
+        nc.scalar.dma_start(out=z[G : 2 * G, :], in_=b.rearrange("(g c) -> g c", c=NB))
+        nc.scalar.activation(out=warm2[:], in_=warm[:], func=ACT.Sigmoid)
+
+        make_identity(nc, ident32[:])
+        make_identity(nc, identb[:])
+        if W_SCALES_ON == "gpsimd":
+            for d in four_planes(nc.gpsimd, F32, tw, W_scales) + two_planes(nc.gpsimd, F32, 0, W_scales, "quadrant"):
+                start(d)
+
+        x32 = x_sb[:].bitcast(F32)
+        xg32 = xg[:].bitcast(F32).rearrange("p (g r u) -> p g r u", g=G, r=P, u=2)
+        for h in range(3):
+            xt = bank(h, [P, 2, 2, P], "xt%d" % h)
+            for gi in range(2):
+                g = 2 * h + gi
+                for u in range(2):
+                    nc.tensor.transpose(xt[:, gi, u, :], x32[:, 256 * g + u : 256 * (g + 1) : 2], ident32[:])
+            nc.scalar.copy(out=xg32[:, 2 * h : 2 * h + 2, :, :], in_=xt[:].rearrange("p g u r -> p g r u"))
+        zt = bank(6, [P, 2, P], "zt")
+        z32 = z[:].bitcast(F32)
+        for u in range(2):
+            nc.tensor.transpose(zt[:, u, :], z32[:, u : 256 : 2], ident32[:])
+
+        def quant(src, codes, plane, h):
+            nc.vector.quantize_mx(
+                out=codes[:, 256 * h : 256 * (h + 1)].bitcast(FP8X4),
+                scales=plane[:, 256 * h : 256 * (h + 1)],
+                in_=src[:, 1024 * h : 1024 * (h + 1)],
+            )
+
+        def prod(h):
+            nc.vector.tensor_tensor(
+                out=xsg[:, 1024 * h : 1024 * (h + 1)].rearrange("p (g r t) -> p g r t", g=2, r=P, t=4),
+                in0=xg[:, 1024 * h : 1024 * (h + 1)].rearrange("p (g r t) -> p g r t", g=2, r=P, t=4),
+                in1=pmt[:, 8 * h : 8 * (h + 1)].rearrange("p (g t) -> p g t", t=4).unsqueeze(2).to_broadcast([P, 2, P, 4]),
+                op=ALU.mult,
+            )
+
+        for h in range(3):
+            quant(xg, xc, xp, h)
+        nc.vector.tensor_copy(
+            out=pmt[:].bitcast(F32).rearrange("p (g u) -> p g u", u=2),
+            in_=zt[:, :, 0:G].rearrange("p u g -> p g u"),
+        )
+        prod(0)
+        prod(1)
+        quant(xsg, xsc, xsp, 0)
+        prod(2)
+        quant(xsg, xsc, xsp, 1)
+        quant(xsg, xsc, xsp, 2)
+
+        def plane_of(which, g):
+            if g < 4:
+                return (tw if which == 0 else tcm), 4 * g
+            return t45, 4 * (g - 4) + 8 * which
+
+        def mx(acc, codes, plane, g, words, wcols, which, ncols):
+            t, k = plane_of(which, g)
+            nc.tensor.matmul_mx(
+                out=acc[:],
+                lhsT=codes[:, P * g : P * (g + 1)].bitcast(FP8X4),
+                lhsT_scale=plane[:, P * g : P * (g + 1)],
+                rhs=words[:, wcols : wcols + NB].bitcast(FP8X4),
+                rhs_scale=t[k:P, ncols : ncols + NB],
+                start=(g == 0),
+                stop=(g == G - 1),
+            )
+
+        accw = [bank(j, [P, NB], "accw%d" % j) for j in range(G)]
+        for g in range(G):
+            for j in range(G):
+                mx(accw[j], xc, xp, g, w_sb[g], NB * j, 0, NB * j)
+            pb = bank(6, [P, NB], "pmb%d" % g)
+            nc.tensor.matmul(out=pb[:], lhsT=identb[:, g : g + 1].to_broadcast([P, P]), rhs=z[:], start=True, stop=True)
+            nc.vector.tensor_tensor(out=xs32[g][:], in0=pb[:], in1=x_sb[:, NB * g : NB * (g + 1)], op=ALU.mult)
+            bb = bank(7, [P, NB], "bb%d" % g)
+            nc.tensor.matmul(out=bb[:], lhsT=identb[:, G + g : G + g + 1].to_broadcast([P, P]), rhs=z[:], start=True, stop=True)
+            nc.scalar.copy(out=ba[g][:], in_=bb[:])
+
+        for j in range(G):
+            nc.vector.tensor_tensor(out=ba[j][:], in0=accw[j][:], in1=ba[j][:], op=ALU.add)
+            nc.scalar.activation(out=ba[j][:], in_=ba[j][:], func=ACT.Sigmoid)
+        for j in range(G):
+            nc.vector.scalar_tensor_tensor(
+                out=ba[j][:], in0=ba[j][:], scalar=0.5 / H, in1=xs32[j][:], op0=ALU.mult, op1=ALU.mult
+            )
+
+        order = [6, 7, 0, 1, 2, 3]
+        nxt = 0
+        for ci, (c0, wd) in enumerate(CHUNKS):
+            nb = wd // NB
+            accs = [bank(order[nxt + i], [P, NB], "accg%d" % (nxt + i)) for i in range(nb)]
+            for g in range(G):
+                for i in range(nb):
+                    mx(accs[i], xsc, xsp, g, c_sb[ci][g], NB * i, 1, c0 + NB * i)
+            for i in range(nb):
+                j = nxt + i
+                nc.vector.tensor_tensor(out=ba[j][:], in0=accs[i][:], in1=ba[j][:], op=ALU.mult)
+                nc.vector.tensor_tensor(out=ba[j][:], in0=ba[j][:], in1=xs32[j][:], op=ALU.add)
+                nc.sync.dma_start(out=out[:, NB * j : NB * (j + 1)], in_=ba[j][:])
+            nxt += nb

@@ -17,10 +17,11 @@ H = 3072
 G = 6
 NB = 512
 FLOPS = 2 * 2 * 128 * 3072 * 3072
-CHUNKS = [(0, 2048), (2048, 512), (2560, 512)]
+CHUNKS = [(0, 1536, 512), (1536, 1024, 512), (2560, 512, 256)]
 W_SCALES_ON = "gpsimd"
 WEAVE = 2
 PIN = True
+SPLIT_LAST = True
 TWO_BY = "row"
 
 
@@ -55,10 +56,12 @@ def tile_neuroplasticitymodule_w_kernel(
         t45 = keep.tile([P, H], U8, name="t45", align_bytes=64)
         tcm = keep.tile([P, H], U8, name="tcm", align_bytes=64)
         w_sb = [keep.tile([P, H], U32, name="w%d" % g, align_bytes=64) for g in range(G)]
-        c_sb = [
-            [keep.tile([P, wd], U32, name="c%d_%d" % (ci, g), align_bytes=64) for g in range(G)]
-            for ci, (c0, wd) in enumerate(CHUNKS)
-        ]
+        pieces = []
+        for ci, (c0, wd, nu) in enumerate(CHUNKS):
+            for g in range(G):
+                cut = nu if (SPLIT_LAST and ci == len(CHUNKS) - 1 and g == G - 1) else wd
+                for s in range(c0, c0 + wd, cut):
+                    pieces.append((g, s, cut, keep.tile([P, cut], U32, name="c%d_%d" % (g, s), align_bytes=64)))
         xg = keep.tile([P, H], BF16, name="xg", align_bytes=64)
         xsg = keep.tile([P, H], BF16, name="xsg", align_bytes=64)
         xc = keep.tile([P, H // 4], U32, name="xc", align_bytes=64)
@@ -100,11 +103,10 @@ def tile_neuroplasticitymodule_w_kernel(
         ] + [
             (
                 nc.sync,
-                c_sb[ci][g][:].bitcast(I32),
-                connectivity_mask_words[g].rearrange("p n t -> p (n t)")[:, 4 * c0 : 4 * (c0 + wd)].bitcast(I32),
+                t[:].bitcast(I32),
+                connectivity_mask_words[g].rearrange("p n t -> p (n t)")[:, 4 * s : 4 * (s + cut)].bitcast(I32),
             )
-            for ci, (c0, wd) in enumerate(CHUNKS)
-            for g in range(G)
+            for (g, s, cut, t) in pieces
         ]
         smalls = []
         if W_SCALES_ON == "sync":
@@ -183,14 +185,14 @@ def tile_neuroplasticitymodule_w_kernel(
                 return (tw if which == 0 else tcm), 4 * g
             return t45, 4 * (g - 4) + 8 * which
 
-        def mx(acc, codes, plane, g, words, wcols, which, ncols):
+        def mx(acc, codes, plane, g, words, wcols, which, ncols, nw=NB):
             t, k = plane_of(which, g)
             nc.tensor.matmul_mx(
                 out=acc[:],
                 lhsT=codes[:, P * g : P * (g + 1)].bitcast(FP8X4),
                 lhsT_scale=plane[:, P * g : P * (g + 1)],
-                rhs=words[:, wcols : wcols + NB].bitcast(FP8X4),
-                rhs_scale=t[k:P, ncols : ncols + NB],
+                rhs=words[:, wcols : wcols + nw].bitcast(FP8X4),
+                rhs_scale=t[k:P, ncols : ncols + nw],
                 start=(g == 0),
                 stop=(g == G - 1),
             )
@@ -214,17 +216,21 @@ def tile_neuroplasticitymodule_w_kernel(
                 out=ba[j][:], in0=ba[j][:], scalar=0.5 / H, in1=xs32[j][:], op0=ALU.mult, op1=ALU.mult
             )
 
-        order = [6, 7, 0, 1, 2, 3]
+        order = [6, 7, 0, 1, 2, 3, 4, 5]
         nxt = 0
-        for ci, (c0, wd) in enumerate(CHUNKS):
-            nb = wd // NB
-            accs = [bank(order[nxt + i], [P, NB], "accg%d" % (nxt + i)) for i in range(nb)]
+        for c0, wd, nu in CHUNKS:
+            units = list(range(c0, c0 + wd, nu))
+            accs = [bank(order[nxt + i], [P, nu], "accg%d" % u) for i, u in enumerate(units)]
+            nxt += len(units)
             for g in range(G):
-                for i in range(nb):
-                    mx(accs[i], xsc, xsp, g, c_sb[ci][g], NB * i, 1, c0 + NB * i)
-            for i in range(nb):
-                j = nxt + i
-                nc.vector.tensor_tensor(out=ba[j][:], in0=accs[i][:], in1=ba[j][:], op=ALU.mult)
-                nc.vector.tensor_tensor(out=ba[j][:], in0=ba[j][:], in1=xs32[j][:], op=ALU.add)
-                nc.sync.dma_start(out=out[:, NB * j : NB * (j + 1)], in_=ba[j][:])
-            nxt += nb
+                for i, u in enumerate(units):
+                    for (pg, s, cut, t) in pieces:
+                        if pg == g and s <= u and u + nu <= s + cut:
+                            mx(accs[i], xsc, xsp, g, t, u - s, 1, u, nu)
+            for i, u in enumerate(units):
+                j = u // NB
+                o = u - NB * j
+                res = keep.tile([P, nu], F32, name="res%d" % u)
+                nc.vector.tensor_tensor(out=res[:], in0=accs[i][:], in1=ba[j][:, o : o + nu], op=ALU.mult)
+                nc.vector.tensor_tensor(out=res[:], in0=res[:], in1=xs32[j][:, o : o + nu], op=ALU.add)
+                nc.sync.dma_start(out=out[:, u : u + nu], in_=res[:])

@@ -21,6 +21,8 @@ CHUNKS = [(0, 1536, 512), (1536, 1024, 512), (2560, 512, 256)]
 W_SCALES_ON = "gpsimd"
 WEAVE = 2
 PIN = True
+MERGE_STORES = True
+ZERO_PLANES = True
 SPLIT_LAST = True
 TWO_BY = "row"
 
@@ -74,8 +76,9 @@ def tile_neuroplasticitymodule_w_kernel(
 
         nc.vector.memset(warm[:], 0.0)
         nc.vector.memset(z[:], 0.0)
-        for t in (tw, t45, tcm):
-            nc.vector.memset(t[:].bitcast(I32), 0)
+        if ZERO_PLANES:
+            for t in (tw, t45, tcm):
+                nc.vector.memset(t[:].bitcast(I32), 0)
 
         def four_planes(eng, dt, t, scales):
             return [
@@ -227,10 +230,19 @@ def tile_neuroplasticitymodule_w_kernel(
                     for (pg, s, cut, t) in pieces:
                         if pg == g and s <= u and u + nu <= s + cut:
                             mx(accs[i], xsc, xsp, g, t, u - s, 1, u, nu)
+            whole = MERGE_STORES and nu == NB
+            if whole:
+                resc = keep.tile([P, wd], F32, name="resc%d" % c0)
             for i, u in enumerate(units):
                 j = u // NB
                 o = u - NB * j
-                res = keep.tile([P, nu], F32, name="res%d" % u)
-                nc.vector.tensor_tensor(out=res[:], in0=accs[i][:], in1=ba[j][:, o : o + nu], op=ALU.mult)
-                nc.vector.tensor_tensor(out=res[:], in0=res[:], in1=xs32[j][:, o : o + nu], op=ALU.add)
-                nc.sync.dma_start(out=out[:, u : u + nu], in_=res[:])
+                if whole:
+                    res = resc[:, u - c0 : u - c0 + nu]
+                else:
+                    res = keep.tile([P, nu], F32, name="res%d" % u)[:]
+                nc.vector.tensor_tensor(out=res, in0=accs[i][:], in1=ba[j][:, o : o + nu], op=ALU.mult)
+                nc.vector.tensor_tensor(out=res, in0=res, in1=xs32[j][:, o : o + nu], op=ALU.add)
+                if not whole:
+                    nc.sync.dma_start(out=out[:, u : u + nu], in_=res)
+            if whole:
+                nc.sync.dma_start(out=out[:, c0 : c0 + wd], in_=resc[:])

@@ -17,14 +17,54 @@ H = 3072
 G = 6
 NB = 512
 FLOPS = 2 * 2 * 128 * 3072 * 3072
-CHUNKS = [(0, 1536, 512), (1536, 1024, 512), (2560, 512, 256)]
-W_SCALES_ON = "gpsimd"
+W_LOADS = [
+    (0, 1, "sync"),
+    (1, 1, "sync"),
+    (2, 1, "sync"),
+    (3, 1, "sync"),
+    (4, 1, "sync"),
+    (5, 1, "sync"),
+]
+CM_LOADS = [
+    (0, 1, 0, 1536, "sync"),
+    (1, 1, 0, 1536, "sync"),
+    (2, 1, 0, 1536, "sync"),
+    (3, 1, 0, 1536, "sync"),
+    (4, 1, 0, 1536, "sync"),
+    (5, 1, 0, 1536, "sync"),
+    (0, 1, 1536, 1024, "sync"),
+    (1, 1, 1536, 1024, "sync"),
+    (2, 1, 1536, 1024, "sync"),
+    (3, 1, 1536, 1024, "sync"),
+    (4, 1, 1536, 1024, "sync"),
+    (5, 1, 1536, 1024, "sync"),
+    (0, 1, 2560, 512, "sync"),
+    (1, 1, 2560, 512, "sync"),
+    (2, 1, 2560, 512, "sync"),
+    (3, 1, 2560, 512, "sync"),
+    (4, 1, 2560, 512, "sync"),
+    (5, 1, 2560, 256, "sync"),
+    (5, 1, 2816, 256, "sync"),
+]
+UNITS = [
+    (0, 512),
+    (512, 512),
+    (1024, 512),
+    (1536, 512),
+    (2048, 512),
+    (2560, 256),
+    (2816, 256),
+]
+BANK_ORDER = [6, 7, 0, 1, 2, 3, 4, 5]
+STORES = [
+    (0, 1536, "sync"),
+    (1536, 1024, "sync"),
+    (2560, 256, "sync"),
+    (2816, 256, "sync"),
+]
 WEAVE = 2
-PIN = True
-MERGE_STORES = True
-ZERO_PLANES = True
-SPLIT_LAST = True
-TWO_BY = "row"
+EPILOGUES = [(0, 512, 1024), (1536, 2048), (2560, 2816)]
+STEPS = (0, 1)
 
 
 def tile_neuroplasticitymodule_w_kernel(
@@ -42,8 +82,8 @@ def tile_neuroplasticitymodule_w_kernel(
     with ExitStack() as ctx:
         keep = ctx.enter_context(tc.tile_pool(name="keep", bufs=1))
         psum = ctx.enter_context(tc.psum_pool(name="psum", bufs=1))
-        if PIN:
-            ctx.enter_context(tc.manual_schedule())
+        ctx.enter_context(tc.manual_schedule())
+        queues = {"sync": nc.sync, "scalar": nc.scalar, "gpsimd": nc.gpsimd}
 
         def bank(i, shape, name):
             return psum.tile(shape, F32, name=name, tag="bank%d" % i)
@@ -57,13 +97,10 @@ def tile_neuroplasticitymodule_w_kernel(
         tw = keep.tile([P, H], U8, name="tw", align_bytes=64)
         t45 = keep.tile([P, H], U8, name="t45", align_bytes=64)
         tcm = keep.tile([P, H], U8, name="tcm", align_bytes=64)
-        w_sb = [keep.tile([P, H], U32, name="w%d" % g, align_bytes=64) for g in range(G)]
-        pieces = []
-        for ci, (c0, wd, nu) in enumerate(CHUNKS):
-            for g in range(G):
-                cut = nu if (SPLIT_LAST and ci == len(CHUNKS) - 1 and g == G - 1) else wd
-                for s in range(c0, c0 + wd, cut):
-                    pieces.append((g, s, cut, keep.tile([P, cut], U32, name="c%d_%d" % (g, s), align_bytes=64)))
+        w_tiles = [keep.tile([P, n * H], U32, name="w%d" % g0, align_bytes=64) for (g0, n, q) in W_LOADS]
+        cm_tiles = [
+            keep.tile([P, n * wd], U32, name="c%d_%d" % (g0, s), align_bytes=64) for (g0, n, s, wd, q) in CM_LOADS
+        ]
         xg = keep.tile([P, H], BF16, name="xg", align_bytes=64)
         xsg = keep.tile([P, H], BF16, name="xsg", align_bytes=64)
         xc = keep.tile([P, H // 4], U32, name="xc", align_bytes=64)
@@ -73,12 +110,12 @@ def tile_neuroplasticitymodule_w_kernel(
         pmt = keep.tile([P, 4 * G], BF16, name="pmt")
         xs32 = [keep.tile([P, NB], F32, name="xs32_%d" % j) for j in range(G)]
         ba = [keep.tile([P, NB], F32, name="ba%d" % j) for j in range(G)]
+        res_tiles = [keep.tile([P, wd], F32, name="res%d" % s) for (s, wd, q) in STORES]
 
         nc.vector.memset(warm[:], 0.0)
         nc.vector.memset(z[:], 0.0)
-        if ZERO_PLANES:
-            for t in (tw, t45, tcm):
-                nc.vector.memset(t[:].bitcast(I32), 0)
+        for t in (tw, t45, tcm):
+            nc.vector.memset(t[:].bitcast(I32), 0)
 
         def four_planes(eng, dt, t, scales):
             return [
@@ -99,33 +136,32 @@ def tile_neuroplasticitymodule_w_kernel(
             ]
 
         def start(d):
-            d[0].dma_start(out=d[1], in_=d[2])
+            queues[d[0]].dma_start(out=d[1], in_=d[2])
 
-        bigs = [
-            (nc.sync, w_sb[g][:].bitcast(I32), W_words[g].rearrange("p n t -> p (n t)").bitcast(I32)) for g in range(G)
-        ] + [
-            (
-                nc.sync,
-                t[:].bitcast(I32),
-                connectivity_mask_words[g].rearrange("p n t -> p (n t)")[:, 4 * s : 4 * (s + cut)].bitcast(I32),
+        def words_load(t, words, g0, n, s, wd, q):
+            dt = I32 if q == "sync" else F32
+            if n == 1:
+                return (
+                    q,
+                    t[:].bitcast(dt),
+                    words[g0].rearrange("p n t -> p (n t)")[:, 4 * s : 4 * (s + wd)].bitcast(dt),
+                )
+            return (
+                q,
+                t[:].bitcast(dt).rearrange("p (g c) -> p g c", g=n),
+                words[g0 : g0 + n].rearrange("g p n t -> p g (n t)")[:, :, 4 * s : 4 * (s + wd)].bitcast(dt),
             )
-            for (g, s, cut, t) in pieces
+
+        bigs = [words_load(t, W_words, g0, n, 0, H, q) for t, (g0, n, q) in zip(w_tiles, W_LOADS)] + [
+            words_load(t, connectivity_mask_words, g0, n, s, wd, q) for t, (g0, n, s, wd, q) in zip(cm_tiles, CM_LOADS)
         ]
-        smalls = []
-        if W_SCALES_ON == "sync":
-            smalls += four_planes(nc.sync, I32, tw, W_scales) + two_planes(nc.sync, I32, 0, W_scales, TWO_BY)
-        smalls += four_planes(nc.sync, I32, tcm, connectivity_mask_scales)
-        smalls += two_planes(nc.sync, I32, 8, connectivity_mask_scales, TWO_BY)
+        smalls = four_planes("sync", I32, tcm, connectivity_mask_scales)
+        smalls += two_planes("sync", I32, 8, connectivity_mask_scales, "row")
 
         nc.sync.dma_start(out=x_sb[:], in_=x)
-        if WEAVE == 0:
-            for d in smalls:
-                start(d)
-            for d in bigs:
-                start(d)
-        else:
-            si = 0
-            for d in bigs:
+        si = 0
+        for d in bigs:
+            if d[0] == "sync":
                 start(d)
                 for d2 in smalls[si : si + WEAVE]:
                     start(d2)
@@ -137,8 +173,10 @@ def tile_neuroplasticitymodule_w_kernel(
 
         make_identity(nc, ident32[:])
         make_identity(nc, identb[:])
-        if W_SCALES_ON == "gpsimd":
-            for d in four_planes(nc.gpsimd, F32, tw, W_scales) + two_planes(nc.gpsimd, F32, 0, W_scales, "quadrant"):
+        for d in four_planes("gpsimd", F32, tw, W_scales) + two_planes("gpsimd", F32, 0, W_scales, "quadrant"):
+            start(d)
+        for d in bigs:
+            if d[0] == "gpsimd":
                 start(d)
 
         x32 = x_sb[:].bitcast(F32)
@@ -201,48 +239,63 @@ def tile_neuroplasticitymodule_w_kernel(
             )
 
         accw = [bank(j, [P, NB], "accw%d" % j) for j in range(G)]
-        for g in range(G):
-            for j in range(G):
-                mx(accw[j], xc, xp, g, w_sb[g], NB * j, 0, NB * j)
-            pb = bank(6, [P, NB], "pmb%d" % g)
-            nc.tensor.matmul(out=pb[:], lhsT=identb[:, g : g + 1].to_broadcast([P, P]), rhs=z[:], start=True, stop=True)
-            nc.vector.tensor_tensor(out=xs32[g][:], in0=pb[:], in1=x_sb[:, NB * g : NB * (g + 1)], op=ALU.mult)
-            bb = bank(7, [P, NB], "bb%d" % g)
-            nc.tensor.matmul(out=bb[:], lhsT=identb[:, G + g : G + g + 1].to_broadcast([P, P]), rhs=z[:], start=True, stop=True)
-            nc.scalar.copy(out=ba[g][:], in_=bb[:])
+        for t, (g0, n, q) in zip(w_tiles, W_LOADS):
+            for g in range(g0, g0 + n):
+                for j in range(G):
+                    mx(accw[j], xc, xp, g, t, H * (g - g0) + NB * j, 0, NB * j)
+                pb = bank(6, [P, NB], "pmb%d" % g)
+                nc.tensor.matmul(out=pb[:], lhsT=identb[:, g : g + 1].to_broadcast([P, P]), rhs=z[:], start=True, stop=True)
+                nc.vector.tensor_tensor(out=xs32[g][:], in0=pb[:], in1=x_sb[:, NB * g : NB * (g + 1)], op=ALU.mult)
+                bb = bank(7, [P, NB], "bb%d" % g)
+                nc.tensor.matmul(
+                    out=bb[:], lhsT=identb[:, G + g : G + g + 1].to_broadcast([P, P]), rhs=z[:], start=True, stop=True
+                )
+                nc.scalar.copy(out=ba[g][:], in_=bb[:])
 
         for j in range(G):
             nc.vector.tensor_tensor(out=ba[j][:], in0=accw[j][:], in1=ba[j][:], op=ALU.add)
             nc.scalar.activation(out=ba[j][:], in_=ba[j][:], func=ACT.Sigmoid)
+        for d in bigs:
+            if d[0] == "scalar":
+                start(d)
         for j in range(G):
             nc.vector.scalar_tensor_tensor(
                 out=ba[j][:], in0=ba[j][:], scalar=0.5 / H, in1=xs32[j][:], op0=ALU.mult, op1=ALU.mult
             )
 
-        order = [6, 7, 0, 1, 2, 3, 4, 5]
-        nxt = 0
-        for c0, wd, nu in CHUNKS:
-            units = list(range(c0, c0 + wd, nu))
-            accs = [bank(order[nxt + i], [P, nu], "accg%d" % u) for i, u in enumerate(units)]
-            nxt += len(units)
-            for g in range(G):
-                for i, u in enumerate(units):
-                    for (pg, s, cut, t) in pieces:
-                        if pg == g and s <= u and u + nu <= s + cut:
-                            mx(accs[i], xsc, xsp, g, t, u - s, 1, u, nu)
-            whole = MERGE_STORES and nu == NB
-            if whole:
-                resc = keep.tile([P, wd], F32, name="resc%d" % c0)
-            for i, u in enumerate(units):
-                j = u // NB
-                o = u - NB * j
-                if whole:
-                    res = resc[:, u - c0 : u - c0 + nu]
-                else:
-                    res = keep.tile([P, nu], F32, name="res%d" % u)[:]
-                nc.vector.tensor_tensor(out=res, in0=accs[i][:], in1=ba[j][:, o : o + nu], op=ALU.mult)
-                nc.vector.tensor_tensor(out=res, in0=res, in1=xs32[j][:, o : o + nu], op=ALU.add)
-                if not whole:
-                    nc.sync.dma_start(out=out[:, u : u + nu], in_=res)
-            if whole:
-                nc.sync.dma_start(out=out[:, c0 : c0 + wd], in_=resc[:])
+        accs = {}
+        summed = set()
+        done = set()
+        widths = dict(UNITS)
+        for t, (g0, n, s, wd, q) in zip(cm_tiles, CM_LOADS):
+            for g in range(g0, g0 + n):
+                for ui, (u, nu) in enumerate(UNITS):
+                    if s <= u and u + nu <= s + wd:
+                        if g == 0:
+                            accs[u] = bank(BANK_ORDER[ui], [P, nu], "accg%d" % u)
+                        mx(accs[u], xsc, xsp, g, t, wd * (g - g0) + u - s, 1, u, nu)
+            if g0 + n == G:
+                for (u, nu) in UNITS:
+                    if s <= u and u + nu <= s + wd:
+                        summed.add(u)
+            for grp in EPILOGUES:
+                if grp[0] in done or not all(u in summed for u in grp):
+                    continue
+                for step in STEPS:
+                    for u in grp:
+                        nu = widths[u]
+                        j = u // NB
+                        o = u - NB * j
+                        for rt, (s0, w0, sq) in zip(res_tiles, STORES):
+                            if s0 <= u and u + nu <= s0 + w0:
+                                res = rt[:, u - s0 : u - s0 + nu]
+                                if step in (0, 2):
+                                    nc.vector.tensor_tensor(out=res, in0=accs[u][:], in1=ba[j][:, o : o + nu], op=ALU.mult)
+                                if step in (1, 2):
+                                    nc.vector.tensor_tensor(out=res, in0=res, in1=xs32[j][:, o : o + nu], op=ALU.add)
+                        if step in (1, 2):
+                            done.add(u)
+                            for rt, (s0, w0, sq) in zip(res_tiles, STORES):
+                                inside = [v for (v, nv) in UNITS if s0 <= v and v < s0 + w0]
+                                if u in inside and all(v in done for v in inside):
+                                    queues[sq].dma_start(out=out[:, s0 : s0 + w0], in_=rt[:])

@@ -65,6 +65,7 @@ STORES = [
 WEAVE = 2
 EPILOGUES = [(0, 512, 1024), (1536, 2048), (2560, 2816)]
 STEPS = (0, 1)
+PARTS = {}
 
 
 def tile_neuroplasticitymodule_w_kernel(
@@ -214,6 +215,15 @@ def tile_neuroplasticitymodule_w_kernel(
             out=pmt[:].bitcast(F32).rearrange("p (g u) -> p g u", u=2),
             in_=zt[:, :, 0:G].rearrange("p u g -> p g u"),
         )
+        for g in range(G):
+            pb = bank((3, 4)[g % 2], [P, NB], "pmb%d" % g)
+            nc.tensor.matmul(out=pb[:], lhsT=identb[:, g : g + 1].to_broadcast([P, P]), rhs=z[:], start=True, stop=True)
+            nc.vector.tensor_tensor(out=xs32[g][:], in0=pb[:], in1=x_sb[:, NB * g : NB * (g + 1)], op=ALU.mult)
+            bb = bank((5, 7)[g % 2], [P, NB], "bb%d" % g)
+            nc.tensor.matmul(
+                out=bb[:], lhsT=identb[:, G + g : G + g + 1].to_broadcast([P, P]), rhs=z[:], start=True, stop=True
+            )
+            nc.scalar.copy(out=ba[g][:], in_=bb[:])
         prod(0)
         prod(1)
         quant(xsg, xsc, xsp, 0)
@@ -243,14 +253,6 @@ def tile_neuroplasticitymodule_w_kernel(
             for g in range(g0, g0 + n):
                 for j in range(G):
                     mx(accw[j], xc, xp, g, t, H * (g - g0) + NB * j, 0, NB * j)
-                pb = bank(6, [P, NB], "pmb%d" % g)
-                nc.tensor.matmul(out=pb[:], lhsT=identb[:, g : g + 1].to_broadcast([P, P]), rhs=z[:], start=True, stop=True)
-                nc.vector.tensor_tensor(out=xs32[g][:], in0=pb[:], in1=x_sb[:, NB * g : NB * (g + 1)], op=ALU.mult)
-                bb = bank(7, [P, NB], "bb%d" % g)
-                nc.tensor.matmul(
-                    out=bb[:], lhsT=identb[:, G + g : G + g + 1].to_broadcast([P, P]), rhs=z[:], start=True, stop=True
-                )
-                nc.scalar.copy(out=ba[g][:], in_=bb[:])
 
         for j in range(G):
             nc.vector.tensor_tensor(out=ba[j][:], in0=accw[j][:], in1=ba[j][:], op=ALU.add)
@@ -285,14 +287,18 @@ def tile_neuroplasticitymodule_w_kernel(
                     for u in grp:
                         nu = widths[u]
                         j = u // NB
-                        o = u - NB * j
+                        cut = nu // PARTS.get(u, 1)
                         for rt, (s0, w0, sq) in zip(res_tiles, STORES):
                             if s0 <= u and u + nu <= s0 + w0:
-                                res = rt[:, u - s0 : u - s0 + nu]
-                                if step in (0, 2):
-                                    nc.vector.tensor_tensor(out=res, in0=accs[u][:], in1=ba[j][:, o : o + nu], op=ALU.mult)
-                                if step in (1, 2):
-                                    nc.vector.tensor_tensor(out=res, in0=res, in1=xs32[j][:, o : o + nu], op=ALU.add)
+                                for c in range(0, nu, cut):
+                                    o = u + c - NB * j
+                                    res = rt[:, u + c - s0 : u + c - s0 + cut]
+                                    if step in (0, 2):
+                                        nc.vector.tensor_tensor(
+                                            out=res, in0=accs[u][:, c : c + cut], in1=ba[j][:, o : o + cut], op=ALU.mult
+                                        )
+                                    if step in (1, 2):
+                                        nc.vector.tensor_tensor(out=res, in0=res, in1=xs32[j][:, o : o + cut], op=ALU.add)
                         if step in (1, 2):
                             done.add(u)
                             for rt, (s0, w0, sq) in zip(res_tiles, STORES):

@@ -26,20 +26,16 @@ W_LOADS = [
     (5, 1, "sync"),
 ]
 CM_LOADS = [
-    (0, 1, 0, 1536, "sync"),
-    (1, 1, 0, 1536, "sync"),
+    (0, 1, 0, 3072, "sync"),
+    (1, 1, 0, 3072, "sync"),
     (2, 1, 0, 1536, "sync"),
     (3, 1, 0, 1536, "sync"),
     (4, 1, 0, 1536, "sync"),
     (5, 1, 0, 1536, "sync"),
-    (0, 1, 1536, 1024, "sync"),
-    (1, 1, 1536, 1024, "sync"),
     (2, 1, 1536, 1024, "sync"),
     (3, 1, 1536, 1024, "sync"),
     (4, 1, 1536, 1024, "sync"),
     (5, 1, 1536, 1024, "sync"),
-    (0, 1, 2560, 512, "sync"),
-    (1, 1, 2560, 512, "sync"),
     (2, 1, 2560, 512, "sync"),
     (3, 1, 2560, 512, "sync"),
     (4, 1, 2560, 512, "sync"),

from contextlib import ExitStack

import concourse.mybir as mybir
from concourse.masks import make_identity

F32 = mybir.dt.float32
BF16 = mybir.dt.bfloat16
U8 = mybir.dt.uint8
U32 = mybir.dt.uint32
I32 = mybir.dt.int32
FP8X4 = mybir.dt.float8_e4m3fn_x4
ALU = mybir.AluOpType
ACT = mybir.ActivationFunctionType

P = 128
H = 3072
G = 6
NB = 512
FLOPS = 2 * 2 * 128 * 3072 * 3072
W_LOADS = [
    (0, 1, "sync"),
    (1, 1, "sync"),
    (2, 1, "sync"),
    (3, 1, "sync"),
    (4, 1, "sync"),
    (5, 1, "sync"),
]
CM_LOADS = [
    (0, 1, 0, 3072, "sync"),
    (1, 1, 0, 3072, "sync"),
    (2, 1, 0, 1536, "sync"),
    (3, 1, 0, 1536, "sync"),
    (4, 1, 0, 1536, "sync"),
    (5, 1, 0, 1536, "sync"),
    (2, 1, 1536, 1024, "sync"),
    (3, 1, 1536, 1024, "sync"),
    (4, 1, 1536, 1024, "sync"),
    (5, 1, 1536, 1024, "sync"),
    (2, 1, 2560, 512, "sync"),
    (3, 1, 2560, 512, "sync"),
    (4, 1, 2560, 512, "sync"),
    (5, 1, 2560, 256, "sync"),
    (5, 1, 2816, 256, "sync"),
]
UNITS = [
    (0, 512),
    (512, 512),
    (1024, 512),
    (1536, 512),
    (2048, 512),
    (2560, 256),
    (2816, 256),
]
BANK_ORDER = [6, 7, 0, 1, 2, 3, 4, 5]
STORES = [
    (0, 1536, "sync"),
    (1536, 1024, "sync"),
    (2560, 256, "sync"),
    (2816, 256, "sync"),
]
WEAVE = 2
EPILOGUES = [(0, 512, 1024), (1536, 2048), (2560, 2816)]
STEPS = (0, 1)
PARTS = {}


def tile_neuroplasticitymodule_w_kernel(
    tc,
    x,
    W_words,
    W_scales,
    b,
    plasticity_modulation,
    connectivity_mask_words,
    connectivity_mask_scales,
    out,
):
    nc = tc.nc
    with ExitStack() as ctx:
        keep = ctx.enter_context(tc.tile_pool(name="keep", bufs=1))
        psum = ctx.enter_context(tc.psum_pool(name="psum", bufs=1))
        ctx.enter_context(tc.manual_schedule())
        queues = {"sync": nc.sync, "scalar": nc.scalar, "gpsimd": nc.gpsimd}

        def bank(i, shape, name):
            return psum.tile(shape, F32, name=name, tag="bank%d" % i)

        x_sb = keep.tile([P, H], BF16, name="x_sb")
        z = keep.tile([P, NB], BF16, name="z")
        warm = keep.tile([P, 1], F32, name="warm")
        warm2 = keep.tile([P, 1], F32, name="warm2")
        ident32 = keep.tile([P, P], F32, name="ident32")
        identb = keep.tile([P, P], BF16, name="identb")
        tw = keep.tile([P, H], U8, name="tw", align_bytes=64)
        t45 = keep.tile([P, H], U8, name="t45", align_bytes=64)
        tcm = keep.tile([P, H], U8, name="tcm", align_bytes=64)
        w_tiles = [keep.tile([P, n * H], U32, name="w%d" % g0, align_bytes=64) for (g0, n, q) in W_LOADS]
        cm_tiles = [
            keep.tile([P, n * wd], U32, name="c%d_%d" % (g0, s), align_bytes=64) for (g0, n, s, wd, q) in CM_LOADS
        ]
        xg = keep.tile([P, H], BF16, name="xg", align_bytes=64)
        xsg = keep.tile([P, H], BF16, name="xsg", align_bytes=64)
        xc = keep.tile([P, H // 4], U32, name="xc", align_bytes=64)
        xp = keep.tile([P, H // 4], U8, name="xp", align_bytes=64)
        xsc = keep.tile([P, H // 4], U32, name="xsc", align_bytes=64)
        xsp = keep.tile([P, H // 4], U8, name="xsp", align_bytes=64)
        pmt = keep.tile([P, 4 * G], BF16, name="pmt")
        xs32 = [keep.tile([P, NB], F32, name="xs32_%d" % j) for j in range(G)]
        ba = [keep.tile([P, NB], F32, name="ba%d" % j) for j in range(G)]
        res_tiles = [keep.tile([P, wd], F32, name="res%d" % s) for (s, wd, q) in STORES]

        nc.vector.memset(warm[:], 0.0)
        nc.vector.memset(z[:], 0.0)
        for t in (tw, t45, tcm):
            nc.vector.memset(t[:].bitcast(I32), 0)

        def four_planes(eng, dt, t, scales):
            return [
                (eng, t[32 * q : 32 * q + 16, :].bitcast(dt), scales[0:4, 4 * q : 4 * q + 4, :].bitcast(dt))
                for q in range(4)
            ]

        def two_planes(eng, dt, k0, scales, by):
            if by == "quadrant":
                return [
                    (eng, t45[32 * q + k0 : 32 * q + k0 + 8, :].bitcast(dt), scales[4:6, 4 * q : 4 * q + 4, :].bitcast(dt))
                    for q in range(4)
                ]
            return [
                (eng, t45[k0 + 4 * (g - 4) + r : P : 32, :].bitcast(dt), scales[g, r : 16 : 4, :].bitcast(dt))
                for g in (4, 5)
                for r in range(4)
            ]

        def start(d):
            queues[d[0]].dma_start(out=d[1], in_=d[2])

        def words_load(t, words, g0, n, s, wd, q):
            dt = I32 if q == "sync" else F32
            if n == 1:
                return (
                    q,
                    t[:].bitcast(dt),
                    words[g0].rearrange("p n t -> p (n t)")[:, 4 * s : 4 * (s + wd)].bitcast(dt),
                )
            return (
                q,
                t[:].bitcast(dt).rearrange("p (g c) -> p g c", g=n),
                words[g0 : g0 + n].rearrange("g p n t -> p g (n t)")[:, :, 4 * s : 4 * (s + wd)].bitcast(dt),
            )

        bigs = [words_load(t, W_words, g0, n, 0, H, q) for t, (g0, n, q) in zip(w_tiles, W_LOADS)] + [
            words_load(t, connectivity_mask_words, g0, n, s, wd, q) for t, (g0, n, s, wd, q) in zip(cm_tiles, CM_LOADS)
        ]
        smalls = four_planes("sync", I32, tcm, connectivity_mask_scales)
        smalls += two_planes("sync", I32, 8, connectivity_mask_scales, "row")

        nc.sync.dma_start(out=x_sb[:], in_=x)
        si = 0
        for d in bigs:
            if d[0] == "sync":
                start(d)
                for d2 in smalls[si : si + WEAVE]:
                    start(d2)
                si += WEAVE

        nc.scalar.dma_start(out=z[0:G, :], in_=plasticity_modulation.rearrange("(g c) -> g c", c=NB))
        nc.scalar.dma_start(out=z[G : 2 * G, :], in_=b.rearrange("(g c) -> g c", c=NB))
        nc.scalar.activation(out=warm2[:], in_=warm[:], func=ACT.Sigmoid)

        make_identity(nc, ident32[:])
        make_identity(nc, identb[:])
        for d in four_planes("gpsimd", F32, tw, W_scales) + two_planes("gpsimd", F32, 0, W_scales, "quadrant"):
            start(d)
        for d in bigs:
            if d[0] == "gpsimd":
                start(d)

        x32 = x_sb[:].bitcast(F32)
        xg32 = xg[:].bitcast(F32).rearrange("p (g r u) -> p g r u", g=G, r=P, u=2)
        for h in range(3):
            xt = bank(h, [P, 2, 2, P], "xt%d" % h)
            for gi in range(2):
                g = 2 * h + gi
                for u in range(2):
                    nc.tensor.transpose(xt[:, gi, u, :], x32[:, 256 * g + u : 256 * (g + 1) : 2], ident32[:])
            nc.scalar.copy(out=xg32[:, 2 * h : 2 * h + 2, :, :], in_=xt[:].rearrange("p g u r -> p g r u"))
        zt = bank(6, [P, 2, P], "zt")
        z32 = z[:].bitcast(F32)
        for u in range(2):
            nc.tensor.transpose(zt[:, u, :], z32[:, u : 256 : 2], ident32[:])

        def quant(src, codes, plane, h):
            nc.vector.quantize_mx(
                out=codes[:, 256 * h : 256 * (h + 1)].bitcast(FP8X4),
                scales=plane[:, 256 * h : 256 * (h + 1)],
                in_=src[:, 1024 * h : 1024 * (h + 1)],
            )

        def prod(h):
            nc.vector.tensor_tensor(
                out=xsg[:, 1024 * h : 1024 * (h + 1)].rearrange("p (g r t) -> p g r t", g=2, r=P, t=4),
                in0=xg[:, 1024 * h : 1024 * (h + 1)].rearrange("p (g r t) -> p g r t", g=2, r=P, t=4),
                in1=pmt[:, 8 * h : 8 * (h + 1)].rearrange("p (g t) -> p g t", t=4).unsqueeze(2).to_broadcast([P, 2, P, 4]),
                op=ALU.mult,
            )

        for h in range(3):
            quant(xg, xc, xp, h)
        nc.vector.tensor_copy(
            out=pmt[:].bitcast(F32).rearrange("p (g u) -> p g u", u=2),
            in_=zt[:, :, 0:G].rearrange("p u g -> p g u"),
        )
        for g in range(G):
            pb = bank((3, 4)[g % 2], [P, NB], "pmb%d" % g)
            nc.tensor.matmul(out=pb[:], lhsT=identb[:, g : g + 1].to_broadcast([P, P]), rhs=z[:], start=True, stop=True)
            nc.vector.tensor_tensor(out=xs32[g][:], in0=pb[:], in1=x_sb[:, NB * g : NB * (g + 1)], op=ALU.mult)
            bb = bank((5, 7)[g % 2], [P, NB], "bb%d" % g)
            nc.tensor.matmul(
                out=bb[:], lhsT=identb[:, G + g : G + g + 1].to_broadcast([P, P]), rhs=z[:], start=True, stop=True
            )
            nc.scalar.copy(out=ba[g][:], in_=bb[:])
        prod(0)
        prod(1)
        quant(xsg, xsc, xsp, 0)
        prod(2)
        quant(xsg, xsc, xsp, 1)
        quant(xsg, xsc, xsp, 2)

        def plane_of(which, g):
            if g < 4:
                return (tw if which == 0 else tcm), 4 * g
            return t45, 4 * (g - 4) + 8 * which

        def mx(acc, codes, plane, g, words, wcols, which, ncols, nw=NB):
            t, k = plane_of(which, g)
            nc.tensor.matmul_mx(
                out=acc[:],
                lhsT=codes[:, P * g : P * (g + 1)].bitcast(FP8X4),
                lhsT_scale=plane[:, P * g : P * (g + 1)],
                rhs=words[:, wcols : wcols + nw].bitcast(FP8X4),
                rhs_scale=t[k:P, ncols : ncols + nw],
                start=(g == 0),
                stop=(g == G - 1),
            )

        accw = [bank(j, [P, NB], "accw%d" % j) for j in range(G)]
        for t, (g0, n, q) in zip(w_tiles, W_LOADS):
            for g in range(g0, g0 + n):
                for j in range(G):
                    mx(accw[j], xc, xp, g, t, H * (g - g0) + NB * j, 0, NB * j)

        for j in range(G):
            nc.vector.tensor_tensor(out=ba[j][:], in0=accw[j][:], in1=ba[j][:], op=ALU.add)
            nc.scalar.activation(out=ba[j][:], in_=ba[j][:], func=ACT.Sigmoid)
        for d in bigs:
            if d[0] == "scalar":
                start(d)
        for j in range(G):
            nc.vector.scalar_tensor_tensor(
                out=ba[j][:], in0=ba[j][:], scalar=0.5 / H, in1=xs32[j][:], op0=ALU.mult, op1=ALU.mult
            )

        accs = {}
        summed = set()
        done = set()
        widths = dict(UNITS)
        for t, (g0, n, s, wd, q) in zip(cm_tiles, CM_LOADS):
            for g in range(g0, g0 + n):
                for ui, (u, nu) in enumerate(UNITS):
                    if s <= u and u + nu <= s + wd:
                        if g == 0:
                            accs[u] = bank(BANK_ORDER[ui], [P, nu], "accg%d" % u)
                        mx(accs[u], xsc, xsp, g, t, wd * (g - g0) + u - s, 1, u, nu)
            if g0 + n == G:
                for (u, nu) in UNITS:
                    if s <= u and u + nu <= s + wd:
                        summed.add(u)
            for grp in EPILOGUES:
                if grp[0] in done or not all(u in summed for u in grp):
                    continue
                for step in STEPS:
                    for u in grp:
                        nu = widths[u]
                        j = u // NB
                        cut = nu // PARTS.get(u, 1)
                        for rt, (s0, w0, sq) in zip(res_tiles, STORES):
                            if s0 <= u and u + nu <= s0 + w0:
                                for c in range(0, nu, cut):
                                    o = u + c - NB * j
                                    res = rt[:, u + c - s0 : u + c - s0 + cut]
                                    if step in (0, 2):
                                        nc.vector.tensor_tensor(
                                            out=res, in0=accs[u][:, c : c + cut], in1=ba[j][:, o : o + cut], op=ALU.mult
                                        )
                                    if step in (1, 2):
                                        nc.vector.tensor_tensor(out=res, in0=res, in1=xs32[j][:, o : o + cut], op=ALU.add)
                        if step in (1, 2):
                            done.add(u)
                            for rt, (s0, w0, sq) in zip(res_tiles, STORES):
                                inside = [v for (v, nv) in UNITS if s0 <= v and v < s0 + w0]
                                if u in inside and all(v in done for v in inside):
                                    queues[sq].dma_start(out=out[:, s0 : s0 + w0], in_=rt[:])
